import numpy as np
import ml_dtypes

BF16 = ml_dtypes.bfloat16


def bf(x):
    return np.asarray(x, np.float32).astype(BF16)


def f32(x):
    return np.asarray(x, np.float32)


def f64(x):
    return np.asarray(x).astype(np.float64)


def striped(idx):
    return np.tile(idx.reshape(-1, 16).T, (8, 1))


C, S, P, L, K, N = 128, 512, 256, 4, 128, 1024
AMP = 5.0
WVALS = (1.0, 2.0, 3.0)


def setup_inputs():
    return {"x": f32(np.random.standard_normal((C, S))), "wgt": f32(np.random.choice(WVALS, size=(1, N))), "w": bf(np.random.standard_normal((C, K)) / np.sqrt(C)), "b": f32(0.1 * np.random.standard_normal((K, 1))), "offs": striped(np.random.permutation(np.tile(np.arange(S), 2))[:N])}


def reference(x, wgt, w, b, offs):
    idx = offs[:16].T.reshape(-1)
    picked = f64(x)[:, idx] * f64(wgt)
    feat = picked.reshape(C, P, L).sum(axis=2) / f64(wgt).reshape(1, P, L).sum(axis=2)
    return AMP * np.tanh(f64(w).T @ feat + f64(b))

@@ -1,0 +1,66 @@
+import concourse.mybir as mybir
+
+F32 = mybir.dt.float32
+BF16 = mybir.dt.bfloat16
+U16 = mybir.dt.uint16
+
+C = 128
+S = 512
+N = 1024
+L = 4
+R = N // L
+K = 128
+AMP = 5.0
+PIECE = 512
+SPANS = PIECE // L
+
+FLOPS = 2 * C * K * R
+
+
+def tile_pretrainedmodel_kernel(tc, x, wgt, w, b, offs, out):
+    nc = tc.nc
+    mult, add = mybir.AluOpType.mult, mybir.AluOpType.add
+    innermost = mybir.AxisListType.X
+    with (
+        tc.tile_pool(name="held", bufs=1) as held,
+        tc.tile_pool(name="work", bufs=2) as work,
+        tc.psum_pool(name="psum", bufs=2) as psum,
+    ):
+        offsets = held.tile([128, N // 16], U16, name="offsets")
+        nc.sync.dma_start(offsets[:], offs)
+        states = held.tile([C, S], F32, name="states")
+        nc.sync.dma_start(states[:], x)
+        weights = held.tile([C, N], F32, name="weights")
+        nc.scalar.dma_start(weights[:], wgt.to_broadcast([C, N]))
+        linear = held.tile([C, K], BF16, name="linear")
+        nc.gpsimd.dma_start(linear[:], w)
+        bias = held.tile([K, 1], F32, name="bias")
+        nc.gpsimd.dma_start(bias[:], b)
+
+        weight_sum = held.tile([C, R], F32, name="weight_sum")
+        nc.vector.tensor_reduce(weight_sum[:], weights[:].rearrange("c (r l) -> c r l", l=L), innermost, add)
+        weight_inv = held.tile([C, R], F32, name="weight_inv")
+        nc.vector.reciprocal(weight_inv[:], weight_sum[:])
+
+        for i in range(N // PIECE):
+            entries = slice(i * PIECE, (i + 1) * PIECE)
+            spans = slice(i * SPANS, (i + 1) * SPANS)
+            picked = work.tile([C, PIECE], F32, name="picked")
+            nc.vector.tensor_tensor(
+                picked[:],
+                states[:].indirect(offsets[:, i * PIECE // 16 : (i + 1) * PIECE // 16]),
+                weights[:, entries],
+                mult,
+            )
+            total = work.tile([C, SPANS], F32, name="total")
+            nc.vector.tensor_reduce(total[:], picked[:].rearrange("c (r l) -> c r l", l=L), innermost, add)
+            feat = work.tile([C, SPANS], BF16, name="feat")
+            nc.vector.tensor_tensor(feat[:], total[:], weight_inv[:, spans], mult)
+
+            logits = psum.tile([K, SPANS], F32, name="logits")
+            nc.tensor.matmul(logits[:], linear[:], feat[:], start=True, stop=True)
+            squashed = work.tile([K, SPANS], F32, name="squashed")
+            nc.scalar.activation(squashed[:], logits[:], mybir.ActivationFunctionType.Tanh, bias=bias[:], scale=1.0)
+            scaled = work.tile([K, SPANS], F32, name="scaled")
+            nc.scalar.mul(scaled[:], squashed[:], AMP)
+            nc.sync.dma_start(out[:, spans], scaled[:])

@@ -1,4 +1,5 @@
 import concourse.mybir as mybir
+from concourse.masks import make_identity
 
 F32 = mybir.dt.float32
 BF16 = mybir.dt.bfloat16
@@ -13,6 +14,7 @@ K = 128
 AMP = 5.0
 PIECE = 512
 SPANS = PIECE // L
+OWN = R // 128
 
 FLOPS = 2 * C * K * R
 
@@ -25,22 +27,38 @@ def tile_pretrainedmodel_kernel(tc, x, wgt, w, b, offs, out):
         tc.tile_pool(name="held", bufs=1) as held,
         tc.tile_pool(name="work", bufs=2) as work,
         tc.psum_pool(name="psum", bufs=2) as psum,
+        tc.psum_pool(name="psum_held", bufs=1) as psum_held,
     ):
         offsets = held.tile([128, N // 16], U16, name="offsets")
         nc.sync.dma_start(offsets[:], offs)
         states = held.tile([C, S], F32, name="states")
         nc.sync.dma_start(states[:], x)
+        own_weights = held.tile([128, OWN * L], F32, name="own_weights")
+        nc.scalar.dma_start(own_weights[:], wgt.rearrange("o (p e) -> (o p) e", e=OWN * L))
         weights = held.tile([C, N], F32, name="weights")
         nc.scalar.dma_start(weights[:], wgt.to_broadcast([C, N]))
         linear = held.tile([C, K], BF16, name="linear")
-        nc.gpsimd.dma_start(linear[:], w)
+        nc.sync.dma_start(linear[:], w)
         bias = held.tile([K, 1], F32, name="bias")
-        nc.gpsimd.dma_start(bias[:], b)
+        nc.sync.dma_start(bias[:], b)
 
-        weight_sum = held.tile([C, R], F32, name="weight_sum")
-        nc.vector.tensor_reduce(weight_sum[:], weights[:].rearrange("c (r l) -> c r l", l=L), innermost, add)
-        weight_inv = held.tile([C, R], F32, name="weight_inv")
-        nc.vector.reciprocal(weight_inv[:], weight_sum[:])
+        own_sum = held.tile([128, OWN], F32, name="own_sum")
+        nc.vector.tensor_reduce(own_sum[:], own_weights[:].rearrange("p (s l) -> p s l", l=L), innermost, add)
+        own_inv = held.tile([128, OWN], F32, name="own_inv")
+        nc.vector.reciprocal(own_inv[:], own_sum[:])
+        identity = held.tile([128, 128], F32, name="identity")
+        make_identity(nc, identity[:])
+        ones = held.tile([128, C], F32, name="ones")
+        nc.gpsimd.memset(ones[:], 1.0)
+        diagonal = held.tile([128, R], F32, name="diagonal")
+        nc.vector.tensor_tensor(
+            diagonal[:].rearrange("p (q s) -> p q s", s=OWN),
+            identity[:].unsqueeze(2).to_broadcast([128, 128, OWN]),
+            own_inv[:].unsqueeze(1).to_broadcast([128, 128, OWN]),
+            mult,
+        )
+        weight_inv = psum_held.tile([C, R], F32, name="weight_inv")
+        nc.tensor.matmul(weight_inv[:], ones[:], diagonal[:], start=True, stop=True)
 
         for i in range(N // PIECE):
             entries = slice(i * PIECE, (i + 1) * PIECE)

@@ -14,7 +14,7 @@ K = 128
 AMP = 5.0
 PIECE = 512
 SPANS = PIECE // L
-OWN = R // 128
+PIECES = N // PIECE
 
 FLOPS = 2 * C * K * R
 
@@ -33,41 +33,41 @@ def tile_pretrainedmodel_kernel(tc, x, wgt, w, b, offs, out):
         nc.sync.dma_start(offsets[:], offs)
         states = held.tile([C, S], F32, name="states")
         nc.sync.dma_start(states[:], x)
-        own_weights = held.tile([128, OWN * L], F32, name="own_weights")
-        nc.scalar.dma_start(own_weights[:], wgt.rearrange("o (p e) -> (o p) e", e=OWN * L))
-        weights = held.tile([C, N], F32, name="weights")
-        nc.scalar.dma_start(weights[:], wgt.to_broadcast([C, N]))
-        linear = held.tile([C, K], BF16, name="linear")
-        nc.sync.dma_start(linear[:], w)
-        bias = held.tile([K, 1], F32, name="bias")
-        nc.sync.dma_start(bias[:], b)
-
-        own_sum = held.tile([128, OWN], F32, name="own_sum")
-        nc.vector.tensor_reduce(own_sum[:], own_weights[:].rearrange("p (s l) -> p s l", l=L), innermost, add)
-        own_inv = held.tile([128, OWN], F32, name="own_inv")
-        nc.vector.reciprocal(own_inv[:], own_sum[:])
-        identity = held.tile([128, 128], F32, name="identity")
-        make_identity(nc, identity[:])
-        ones = held.tile([128, C], F32, name="ones")
-        nc.gpsimd.memset(ones[:], 1.0)
-        diagonal = held.tile([128, R], F32, name="diagonal")
-        nc.vector.tensor_tensor(
-            diagonal[:].rearrange("p (q s) -> p q s", s=OWN),
-            identity[:].unsqueeze(2).to_broadcast([128, 128, OWN]),
-            own_inv[:].unsqueeze(1).to_broadcast([128, 128, OWN]),
-            mult,
+        own_weights = held.tile([SPANS, PIECES * L], F32, name="own_weights")
+        nc.scalar.dma_start(
+            own_weights[:].rearrange("p (i l) -> p i l", l=L), wgt.rearrange("o (i p l) -> (o p) i l", i=PIECES, l=L)
         )
-        weight_inv = psum_held.tile([C, R], F32, name="weight_inv")
-        nc.tensor.matmul(weight_inv[:], ones[:], diagonal[:], start=True, stop=True)
+        weights = [held.tile([C, PIECE], F32, name=f"weights{i}") for i in range(PIECES)]
+        nc.scalar.dma_start(weights[0][:], wgt[:, 0:PIECE].to_broadcast([C, PIECE]))
+        nc.sync.dma_start(weights[1][:], wgt[:, PIECE : 2 * PIECE].to_broadcast([C, PIECE]))
+        linear = held.tile([C, K], BF16, name="linear")
+        nc.scalar.dma_start(linear[:], w)
+        bias = held.tile([K, 1], F32, name="bias")
+        nc.scalar.dma_start(bias[:], b)
 
-        for i in range(N // PIECE):
-            entries = slice(i * PIECE, (i + 1) * PIECE)
+        own_sum = held.tile([SPANS, PIECES], F32, name="own_sum")
+        nc.vector.tensor_reduce(own_sum[:], own_weights[:].rearrange("p (i l) -> p i l", l=L), innermost, add)
+        own_inv = held.tile([SPANS, PIECES], F32, name="own_inv")
+        nc.vector.reciprocal(own_inv[:], own_sum[:])
+        identity = held.tile([SPANS, SPANS], F32, name="identity")
+        make_identity(nc, identity[:])
+        weight_inv = psum_held.tile([C, R], F32, name="weight_inv")
+        for i in range(PIECES):
+            nc.tensor.matmul(
+                weight_inv[:, i * SPANS : (i + 1) * SPANS],
+                own_inv[:, i : i + 1].to_broadcast([SPANS, C]),
+                identity[:],
+                start=True,
+                stop=True,
+            )
+
+        for i in range(PIECES):
             spans = slice(i * SPANS, (i + 1) * SPANS)
             picked = work.tile([C, PIECE], F32, name="picked")
             nc.vector.tensor_tensor(
                 picked[:],
                 states[:].indirect(offsets[:, i * PIECE // 16 : (i + 1) * PIECE // 16]),
-                weights[:, entries],
+                weights[i][:],
                 mult,
             )
             total = work.tile([C, SPANS], F32, name="total")

@@ -51,29 +51,31 @@ def tile_pretrainedmodel_kernel(tc, x, wgt, w, b, offs, out):
         nc.vector.reciprocal(own_inv[:], own_sum[:])
         identity = held.tile([SPANS, SPANS], F32, name="identity")
         make_identity(nc, identity[:])
-        weight_inv = psum_held.tile([C, R], F32, name="weight_inv")
+        weight_inv = [psum_held.tile([C, SPANS], F32, name=f"weight_inv{i}") for i in range(PIECES)]
         for i in range(PIECES):
             nc.tensor.matmul(
-                weight_inv[:, i * SPANS : (i + 1) * SPANS],
+                weight_inv[i][:],
                 own_inv[:, i : i + 1].to_broadcast([SPANS, C]),
                 identity[:],
                 start=True,
                 stop=True,
             )
 
+        picked = [held.tile([C, PIECE], F32, name=f"picked{i}") for i in range(PIECES)]
         for i in range(PIECES):
-            spans = slice(i * SPANS, (i + 1) * SPANS)
-            picked = work.tile([C, PIECE], F32, name="picked")
             nc.vector.tensor_tensor(
-                picked[:],
+                picked[i][:],
                 states[:].indirect(offsets[:, i * PIECE // 16 : (i + 1) * PIECE // 16]),
                 weights[i][:],
                 mult,
             )
+
+        for i in range(PIECES):
+            spans = slice(i * SPANS, (i + 1) * SPANS)
             total = work.tile([C, SPANS], F32, name="total")
-            nc.vector.tensor_reduce(total[:], picked[:].rearrange("c (r l) -> c r l", l=L), innermost, add)
+            nc.vector.tensor_reduce(total[:], picked[i][:].rearrange("c (r l) -> c r l", l=L), innermost, add)
             feat = work.tile([C, SPANS], BF16, name="feat")
-            nc.vector.tensor_tensor(feat[:], total[:], weight_inv[:, spans], mult)
+            nc.vector.tensor_tensor(feat[:], total[:], weight_inv[i][:], mult)
 
             logits = psum.tile([K, SPANS], F32, name="logits")
             nc.tensor.matmul(logits[:], linear[:], feat[:], start=True, stop=True)

@@ -37,13 +37,17 @@ def tile_pretrainedmodel_kernel(tc, x, wgt, w, b, offs, out):
         nc.scalar.dma_start(
             own_weights[:].rearrange("p (i l) -> p i l", l=L), wgt.rearrange("o (i p l) -> (o p) i l", i=PIECES, l=L)
         )
+        bias = held.tile([K, 1], F32, name="bias")
+        nc.scalar.dma_start(bias[:], b)
         weights = [held.tile([C, PIECE], F32, name=f"weights{i}") for i in range(PIECES)]
         nc.scalar.dma_start(weights[0][:], wgt[:, 0:PIECE].to_broadcast([C, PIECE]))
         nc.sync.dma_start(weights[1][:], wgt[:, PIECE : 2 * PIECE].to_broadcast([C, PIECE]))
         linear = held.tile([C, K], BF16, name="linear")
         nc.scalar.dma_start(linear[:], w)
-        bias = held.tile([K, 1], F32, name="bias")
-        nc.scalar.dma_start(bias[:], b)
+
+        scratch = held.tile([K, 1], F32, name="scratch")
+        nc.vector.memset(scratch[:], 0.0)
+        nc.scalar.activation(scratch[:], scratch[:], mybir.ActivationFunctionType.Tanh)
 
         own_sum = held.tile([SPANS, PIECES], F32, name="own_sum")
         nc.vector.tensor_reduce(own_sum[:], own_weights[:].rearrange("p (i l) -> p i l", l=L), innermost, add)

@@ -29,25 +29,21 @@ def tile_pretrainedmodel_kernel(tc, x, wgt, w, b, offs, out):
         tc.psum_pool(name="psum", bufs=2) as psum,
         tc.psum_pool(name="psum_held", bufs=1) as psum_held,
     ):
-        offsets = held.tile([128, N // 16], U16, name="offsets")
-        nc.sync.dma_start(offsets[:], offs)
         states = held.tile([C, S], F32, name="states")
         nc.sync.dma_start(states[:], x)
+        weights = [held.tile([C, PIECE], F32, name=f"weights{i}") for i in range(PIECES)]
+        nc.scalar.dma_start(weights[0][:], wgt[:, 0:PIECE].to_broadcast([C, PIECE]))
+        offsets = held.tile([128, N // 16], U16, name="offsets")
+        nc.sync.dma_start(offsets[:], offs)
+        nc.sync.dma_start(weights[1][:], wgt[:, PIECE : 2 * PIECE].to_broadcast([C, PIECE]))
         own_weights = held.tile([SPANS, PIECES * L], F32, name="own_weights")
         nc.scalar.dma_start(
             own_weights[:].rearrange("p (i l) -> p i l", l=L), wgt.rearrange("o (i p l) -> (o p) i l", i=PIECES, l=L)
         )
-        bias = held.tile([K, 1], F32, name="bias")
-        nc.scalar.dma_start(bias[:], b)
-        weights = [held.tile([C, PIECE], F32, name=f"weights{i}") for i in range(PIECES)]
-        nc.scalar.dma_start(weights[0][:], wgt[:, 0:PIECE].to_broadcast([C, PIECE]))
-        nc.sync.dma_start(weights[1][:], wgt[:, PIECE : 2 * PIECE].to_broadcast([C, PIECE]))
         linear = held.tile([C, K], BF16, name="linear")
         nc.scalar.dma_start(linear[:], w)
-
-        scratch = held.tile([K, 1], F32, name="scratch")
-        nc.vector.memset(scratch[:], 0.0)
-        nc.scalar.activation(scratch[:], scratch[:], mybir.ActivationFunctionType.Tanh)
+        bias = held.tile([K, 1], F32, name="bias")
+        nc.scalar.dma_start(bias[:], b)
 
         own_sum = held.tile([SPANS, PIECES], F32, name="own_sum")
         nc.vector.tensor_reduce(own_sum[:], own_weights[:].rearrange("p (i l) -> p i l", l=L), innermost, add)

@@ -12,9 +12,8 @@ L = 4
 R = N // L
 K = 128
 AMP = 5.0
-PIECE = 512
-SPANS = PIECE // L
-PIECES = N // PIECE
+PIECE = S
+OWN = R // 128
 
 FLOPS = 2 * C * K * R
 
@@ -23,64 +22,54 @@ def tile_pretrainedmodel_kernel(tc, x, wgt, w, b, offs, out):
     nc = tc.nc
     mult, add = mybir.AluOpType.mult, mybir.AluOpType.add
     innermost = mybir.AxisListType.X
-    with (
-        tc.tile_pool(name="held", bufs=1) as held,
-        tc.tile_pool(name="work", bufs=2) as work,
-        tc.psum_pool(name="psum", bufs=2) as psum,
-        tc.psum_pool(name="psum_held", bufs=1) as psum_held,
-    ):
-        states = held.tile([C, S], F32, name="states")
-        nc.sync.dma_start(states[:], x)
-        weights = [held.tile([C, PIECE], F32, name=f"weights{i}") for i in range(PIECES)]
-        nc.scalar.dma_start(weights[0][:], wgt[:, 0:PIECE].to_broadcast([C, PIECE]))
-        offsets = held.tile([128, N // 16], U16, name="offsets")
+    with tc.tile_pool(name="sbuf", bufs=1) as sbuf, tc.psum_pool(name="psum", bufs=1) as psum:
+        offsets = sbuf.tile([128, N // 16], U16, name="offsets")
         nc.sync.dma_start(offsets[:], offs)
-        nc.sync.dma_start(weights[1][:], wgt[:, PIECE : 2 * PIECE].to_broadcast([C, PIECE]))
-        own_weights = held.tile([SPANS, PIECES * L], F32, name="own_weights")
-        nc.scalar.dma_start(
-            own_weights[:].rearrange("p (i l) -> p i l", l=L), wgt.rearrange("o (i p l) -> (o p) i l", i=PIECES, l=L)
-        )
-        linear = held.tile([C, K], BF16, name="linear")
+        states = sbuf.tile([C, S], F32, name="states")
+        nc.sync.dma_start(states[:], x)
+        own_weights = sbuf.tile([128, OWN * L], F32, name="own_weights")
+        nc.scalar.dma_start(own_weights[:], wgt.rearrange("o (p e) -> (o p) e", e=OWN * L))
+        weights = sbuf.tile([C, N], F32, name="weights")
+        nc.scalar.dma_start(weights[:, 0:PIECE], wgt[:, 0:PIECE].to_broadcast([C, PIECE]))
+        nc.sync.dma_start(weights[:, PIECE:N], wgt[:, PIECE:N].to_broadcast([C, N - PIECE]))
+        linear = sbuf.tile([C, K], BF16, name="linear")
         nc.scalar.dma_start(linear[:], w)
-        bias = held.tile([K, 1], F32, name="bias")
+        bias = sbuf.tile([K, 1], F32, name="bias")
         nc.scalar.dma_start(bias[:], b)
 
-        own_sum = held.tile([SPANS, PIECES], F32, name="own_sum")
-        nc.vector.tensor_reduce(own_sum[:], own_weights[:].rearrange("p (i l) -> p i l", l=L), innermost, add)
-        own_inv = held.tile([SPANS, PIECES], F32, name="own_inv")
+        own_sum = sbuf.tile([128, OWN], F32, name="own_sum")
+        nc.vector.tensor_reduce(own_sum[:], own_weights[:].rearrange("p (s l) -> p s l", l=L), innermost, add)
+        own_inv = sbuf.tile([128, OWN], F32, name="own_inv")
         nc.vector.reciprocal(own_inv[:], own_sum[:])
-        identity = held.tile([SPANS, SPANS], F32, name="identity")
+        identity = sbuf.tile([128, 128], F32, name="identity")
         make_identity(nc, identity[:])
-        weight_inv = [psum_held.tile([C, SPANS], F32, name=f"weight_inv{i}") for i in range(PIECES)]
-        for i in range(PIECES):
+        weight_inv = psum.tile([C, R], F32, name="weight_inv")
+        for s in range(OWN):
             nc.tensor.matmul(
-                weight_inv[i][:],
-                own_inv[:, i : i + 1].to_broadcast([SPANS, C]),
+                weight_inv[:].rearrange("c (q s) -> c q s", s=OWN)[:, :, s],
+                own_inv[:, s : s + 1].to_broadcast([128, C]),
                 identity[:],
                 start=True,
                 stop=True,
             )
 
-        picked = [held.tile([C, PIECE], F32, name=f"picked{i}") for i in range(PIECES)]
-        for i in range(PIECES):
+        picked = sbuf.tile([C, N], F32, name="picked")
+        for start in range(0, N, PIECE):
             nc.vector.tensor_tensor(
-                picked[i][:],
-                states[:].indirect(offsets[:, i * PIECE // 16 : (i + 1) * PIECE // 16]),
-                weights[i][:],
+                picked[:, start : start + PIECE],
+                states[:].indirect(offsets[:, start // 16 : (start + PIECE) // 16]),
+                weights[:, start : start + PIECE],
                 mult,
             )
+        total = sbuf.tile([C, R], F32, name="total")
+        nc.vector.tensor_reduce(total[:], picked[:].rearrange("c (r l) -> c r l", l=L), innermost, add)
+        feat = sbuf.tile([C, R], BF16, name="feat")
+        nc.vector.tensor_tensor(feat[:], total[:], weight_inv[:], mult)
 
-        for i in range(PIECES):
-            spans = slice(i * SPANS, (i + 1) * SPANS)
-            total = work.tile([C, SPANS], F32, name="total")
-            nc.vector.tensor_reduce(total[:], picked[i][:].rearrange("c (r l) -> c r l", l=L), innermost, add)
-            feat = work.tile([C, SPANS], BF16, name="feat")
-            nc.vector.tensor_tensor(feat[:], total[:], weight_inv[i][:], mult)
-
-            logits = psum.tile([K, SPANS], F32, name="logits")
-            nc.tensor.matmul(logits[:], linear[:], feat[:], start=True, stop=True)
-            squashed = work.tile([K, SPANS], F32, name="squashed")
-            nc.scalar.activation(squashed[:], logits[:], mybir.ActivationFunctionType.Tanh, bias=bias[:], scale=1.0)
-            scaled = work.tile([K, SPANS], F32, name="scaled")
-            nc.scalar.mul(scaled[:], squashed[:], AMP)
-            nc.sync.dma_start(out[:, spans], scaled[:])
+        logits = psum.tile([K, R], F32, name="logits")
+        nc.tensor.matmul(logits[:], linear[:], feat[:], start=True, stop=True)
+        squashed = sbuf.tile([K, R], F32, name="squashed")
+        nc.scalar.activation(squashed[:], logits[:], mybir.ActivationFunctionType.Tanh, bias=bias[:], scale=1.0)
+        scaled = sbuf.tile([K, R], F32, name="scaled")
+        nc.scalar.mul(scaled[:], squashed[:], AMP)
+        nc.sync.dma_start(out, scaled[:])

@@ -12,8 +12,9 @@ L = 4
 R = N // L
 K = 128
 AMP = 5.0
-PIECE = S
-OWN = R // 128
+PIECE = 512
+SPANS = PIECE // L
+PIECES = N // PIECE
 
 FLOPS = 2 * C * K * R
 
@@ -22,54 +23,62 @@ def tile_pretrainedmodel_kernel(tc, x, wgt, w, b, offs, out):
     nc = tc.nc
     mult, add = mybir.AluOpType.mult, mybir.AluOpType.add
     innermost = mybir.AxisListType.X
-    with tc.tile_pool(name="sbuf", bufs=1) as sbuf, tc.psum_pool(name="psum", bufs=1) as psum:
-        offsets = sbuf.tile([128, N // 16], U16, name="offsets")
+    with (
+        tc.tile_pool(name="held", bufs=1) as held,
+        tc.tile_pool(name="work", bufs=2) as work,
+        tc.psum_pool(name="psum", bufs=2) as psum,
+        tc.psum_pool(name="psum_held", bufs=1) as psum_held,
+    ):
+        offsets = held.tile([128, N // 16], U16, name="offsets")
         nc.sync.dma_start(offsets[:], offs)
-        states = sbuf.tile([C, S], F32, name="states")
+        states = held.tile([C, S], F32, name="states")
         nc.sync.dma_start(states[:], x)
-        own_weights = sbuf.tile([128, OWN * L], F32, name="own_weights")
-        nc.scalar.dma_start(own_weights[:], wgt.rearrange("o (p e) -> (o p) e", e=OWN * L))
-        weights = sbuf.tile([C, N], F32, name="weights")
-        nc.scalar.dma_start(weights[:, 0:PIECE], wgt[:, 0:PIECE].to_broadcast([C, PIECE]))
-        nc.sync.dma_start(weights[:, PIECE:N], wgt[:, PIECE:N].to_broadcast([C, N - PIECE]))
-        linear = sbuf.tile([C, K], BF16, name="linear")
-        nc.scalar.dma_start(linear[:], w)
-        bias = sbuf.tile([K, 1], F32, name="bias")
-        nc.scalar.dma_start(bias[:], b)
+        own_weights = held.tile([SPANS, PIECES * L], F32, name="own_weights")
+        nc.scalar.dma_start(
+            own_weights[:].rearrange("p (i l) -> p i l", l=L), wgt.rearrange("o (i p l) -> (o p) i l", i=PIECES, l=L)
+        )
+        weights = held.tile([C, N], F32, name="weights")
+        nc.scalar.dma_start(weights[:], wgt.to_broadcast([C, N]))
+        linear = held.tile([C, K], BF16, name="linear")
+        nc.sync.dma_start(linear[:], w)
+        bias = held.tile([K, 1], F32, name="bias")
+        nc.sync.dma_start(bias[:], b)
 
-        own_sum = sbuf.tile([128, OWN], F32, name="own_sum")
-        nc.vector.tensor_reduce(own_sum[:], own_weights[:].rearrange("p (s l) -> p s l", l=L), innermost, add)
-        own_inv = sbuf.tile([128, OWN], F32, name="own_inv")
+        own_sum = held.tile([SPANS, PIECES], F32, name="own_sum")
+        nc.vector.tensor_reduce(own_sum[:], own_weights[:].rearrange("p (i l) -> p i l", l=L), innermost, add)
+        own_inv = held.tile([SPANS, PIECES], F32, name="own_inv")
         nc.vector.reciprocal(own_inv[:], own_sum[:])
-        identity = sbuf.tile([128, 128], F32, name="identity")
+        identity = held.tile([SPANS, SPANS], F32, name="identity")
         make_identity(nc, identity[:])
-        weight_inv = psum.tile([C, R], F32, name="weight_inv")
-        for s in range(OWN):
+        weight_inv = psum_held.tile([C, R], F32, name="weight_inv")
+        for i in range(PIECES):
             nc.tensor.matmul(
-                weight_inv[:].rearrange("c (q s) -> c q s", s=OWN)[:, :, s],
-                own_inv[:, s : s + 1].to_broadcast([128, C]),
+                weight_inv[:, i * SPANS : (i + 1) * SPANS],
+                own_inv[:, i : i + 1].to_broadcast([SPANS, C]),
                 identity[:],
                 start=True,
                 stop=True,
             )
 
-        picked = sbuf.tile([C, N], F32, name="picked")
-        for start in range(0, N, PIECE):
+        for i in range(PIECES):
+            entries = slice(i * PIECE, (i + 1) * PIECE)
+            spans = slice(i * SPANS, (i + 1) * SPANS)
+            picked = work.tile([C, PIECE], F32, name="picked")
             nc.vector.tensor_tensor(
-                picked[:, start : start + PIECE],
-                states[:].indirect(offsets[:, start // 16 : (start + PIECE) // 16]),
-                weights[:, start : start + PIECE],
+                picked[:],
+                states[:].indirect(offsets[:, i * PIECE // 16 : (i + 1) * PIECE // 16]),
+                weights[:, entries],
                 mult,
             )
-        total = sbuf.tile([C, R], F32, name="total")
-        nc.vector.tensor_reduce(total[:], picked[:].rearrange("c (r l) -> c r l", l=L), innermost, add)
-        feat = sbuf.tile([C, R], BF16, name="feat")
-        nc.vector.tensor_tensor(feat[:], total[:], weight_inv[:], mult)
+            total = work.tile([C, SPANS], F32, name="total")
+            nc.vector.tensor_reduce(total[:], picked[:].rearrange("c (r l) -> c r l", l=L), innermost, add)
+            feat = work.tile([C, SPANS], BF16, name="feat")
+            nc.vector.tensor_tensor(feat[:], total[:], weight_inv[:, spans], mult)
 
-        logits = psum.tile([K, R], F32, name="logits")
-        nc.tensor.matmul(logits[:], linear[:], feat[:], start=True, stop=True)
-        squashed = sbuf.tile([K, R], F32, name="squashed")
-        nc.scalar.activation(squashed[:], logits[:], mybir.ActivationFunctionType.Tanh, bias=bias[:], scale=1.0)
-        scaled = sbuf.tile([K, R], F32, name="scaled")
-        nc.scalar.mul(scaled[:], squashed[:], AMP)
-        nc.sync.dma_start(out, scaled[:])
+            logits = psum.tile([K, SPANS], F32, name="logits")
+            nc.tensor.matmul(logits[:], linear[:], feat[:], start=True, stop=True)
+            squashed = work.tile([K, SPANS], F32, name="squashed")
+            nc.scalar.activation(squashed[:], logits[:], mybir.ActivationFunctionType.Tanh, bias=bias[:], scale=1.0)
+            scaled = work.tile([K, SPANS], F32, name="scaled")
+            nc.scalar.mul(scaled[:], squashed[:], AMP)
+            nc.sync.dma_start(out[:, spans], scaled[:])

@@ -29,16 +29,16 @@ def tile_pretrainedmodel_kernel(tc, x, wgt, w, b, offs, out):
         tc.psum_pool(name="psum", bufs=2) as psum,
         tc.psum_pool(name="psum_held", bufs=1) as psum_held,
     ):
+        weights = held.tile([C, N], F32, name="weights")
+        nc.sync.dma_start(weights[:], wgt.to_broadcast([C, N]))
         offsets = held.tile([128, N // 16], U16, name="offsets")
         nc.sync.dma_start(offsets[:], offs)
-        states = held.tile([C, S], F32, name="states")
-        nc.sync.dma_start(states[:], x)
         own_weights = held.tile([SPANS, PIECES * L], F32, name="own_weights")
         nc.scalar.dma_start(
             own_weights[:].rearrange("p (i l) -> p i l", l=L), wgt.rearrange("o (i p l) -> (o p) i l", i=PIECES, l=L)
         )
-        weights = held.tile([C, N], F32, name="weights")
-        nc.scalar.dma_start(weights[:], wgt.to_broadcast([C, N]))
+        states = held.tile([C, S], F32, name="states")
+        nc.scalar.dma_start(states[:], x)
         linear = held.tile([C, K], BF16, name="linear")
         nc.sync.dma_start(linear[:], w)
         bias = held.tile([K, 1], F32, name="bias")

@@ -80,5 +80,5 @@ def tile_pretrainedmodel_kernel(tc, x, wgt, w, b, offs, out):
             squashed = work.tile([K, SPANS], F32, name="squashed")
             nc.scalar.activation(squashed[:], logits[:], mybir.ActivationFunctionType.Tanh, bias=bias[:], scale=1.0)
             scaled = work.tile([K, SPANS], F32, name="scaled")
-            nc.scalar.mul(scaled[:], squashed[:], AMP)
+            nc.vector.tensor_scalar_mul(scaled[:], squashed[:], AMP)
             nc.sync.dma_start(out[:, spans], scaled[:])

@@ -29,49 +29,62 @@ def tile_pretrainedmodel_kernel(tc, x, wgt, w, b, offs, out):
         tc.psum_pool(name="psum", bufs=2) as psum,
         tc.psum_pool(name="psum_held", bufs=1) as psum_held,
     ):
-        weights = held.tile([C, N], F32, name="weights")
-        nc.sync.dma_start(weights[:], wgt.to_broadcast([C, N]))
-        offsets = held.tile([128, N // 16], U16, name="offsets")
-        nc.sync.dma_start(offsets[:], offs)
-        own_weights = held.tile([SPANS, PIECES * L], F32, name="own_weights")
-        nc.scalar.dma_start(
-            own_weights[:].rearrange("p (i l) -> p i l", l=L), wgt.rearrange("o (i p l) -> (o p) i l", i=PIECES, l=L)
-        )
+        own_weights = held.tile([SPANS, PIECES, L], F32, name="own_weights")
+        nc.sync.dma_start(own_weights[:], wgt.rearrange("o (i p l) -> (o p) i l", i=PIECES, l=L))
         states = held.tile([C, S], F32, name="states")
         nc.scalar.dma_start(states[:], x)
+        offsets = held.tile([128, N // 16], U16, name="offsets")
+        nc.sync.dma_start(offsets[:], offs)
         linear = held.tile([C, K], BF16, name="linear")
         nc.sync.dma_start(linear[:], w)
         bias = held.tile([K, 1], F32, name="bias")
         nc.sync.dma_start(bias[:], b)
 
-        own_sum = held.tile([SPANS, PIECES], F32, name="own_sum")
-        nc.vector.tensor_reduce(own_sum[:], own_weights[:].rearrange("p (i l) -> p i l", l=L), innermost, add)
-        own_inv = held.tile([SPANS, PIECES], F32, name="own_inv")
-        nc.vector.reciprocal(own_inv[:], own_sum[:])
+        zero = held.tile([128, 1], F32, name="zero")
+        nc.vector.memset(zero[:], 0.0)
+        warm = held.tile([128, 1], F32, name="warm")
+        nc.scalar.activation(warm[:], zero[:], mybir.ActivationFunctionType.Tanh)
+
         identity = held.tile([SPANS, SPANS], F32, name="identity")
         make_identity(nc, identity[:])
+        weights = []
+        for i in range(PIECES):
+            spread = psum_held.tile([C, SPANS, L], F32, name=f"spread{i}")
+            for l in range(L):
+                nc.tensor.transpose(
+                    spread[:, :, l], own_weights[:, i, l : l + 1].to_broadcast([SPANS, C]), identity[:]
+                )
+            row = held.tile([C, PIECE], F32, name=f"weights{i}")
+            if i == 0:
+                nc.vector.tensor_copy(row[:], spread[:].rearrange("c r l -> c (r l)"))
+            else:
+                nc.scalar.copy(row[:], spread[:].rearrange("c r l -> c (r l)"))
+            weights.append(row)
+
+        own_sum = held.tile([SPANS, PIECES], F32, name="own_sum")
+        nc.vector.tensor_reduce(own_sum[:], own_weights[:], innermost, add)
+        own_inv = held.tile([SPANS, PIECES], F32, name="own_inv")
+        nc.vector.reciprocal(own_inv[:], own_sum[:])
         weight_inv = psum_held.tile([C, R], F32, name="weight_inv")
         for i in range(PIECES):
-            nc.tensor.matmul(
+            nc.tensor.transpose(
                 weight_inv[:, i * SPANS : (i + 1) * SPANS],
                 own_inv[:, i : i + 1].to_broadcast([SPANS, C]),
                 identity[:],
-                start=True,
-                stop=True,
             )
 
+        picked = []
         for i in range(PIECES):
-            entries = slice(i * PIECE, (i + 1) * PIECE)
-            spans = slice(i * SPANS, (i + 1) * SPANS)
-            picked = work.tile([C, PIECE], F32, name="picked")
+            product = held.tile([C, PIECE], F32, name=f"picked{i}")
             nc.vector.tensor_tensor(
-                picked[:],
-                states[:].indirect(offsets[:, i * PIECE // 16 : (i + 1) * PIECE // 16]),
-                weights[:, entries],
-                mult,
+                product[:], states[:].indirect(offsets[:, i * PIECE // 16 : (i + 1) * PIECE // 16]), weights[i][:], mult
             )
+            picked.append(product)
+
+        for i in range(PIECES):
+            spans = slice(i * SPANS, (i + 1) * SPANS)
             total = work.tile([C, SPANS], F32, name="total")
-            nc.vector.tensor_reduce(total[:], picked[:].rearrange("c (r l) -> c r l", l=L), innermost, add)
+            nc.vector.tensor_reduce(total[:], picked[i][:].rearrange("c (r l) -> c r l", l=L), innermost, add)
             feat = work.tile([C, SPANS], BF16, name="feat")
             nc.vector.tensor_tensor(feat[:], total[:], weight_inv[:, spans], mult)
 

@@ -12,9 +12,11 @@ L = 4
 R = N // L
 K = 128
 AMP = 5.0
-PIECE = 512
-SPANS = PIECE // L
-PIECES = N // PIECE
+SPANS = R // 2
+HALF = SPANS * L
+P = 128
+FIRST_HALF = ((0, P), (P, 2 * P), (2 * P, 4 * P))
+SECOND_HALF = ((HALF, HALF + 2 * P), (HALF + 2 * P, HALF + 4 * P))
 
 FLOPS = 2 * C * K * R
 
@@ -29,8 +31,11 @@ def tile_pretrainedmodel_kernel(tc, x, wgt, w, b, offs, out):
         tc.psum_pool(name="psum", bufs=2) as psum,
         tc.psum_pool(name="psum_held", bufs=1) as psum_held,
     ):
-        own_weights = held.tile([SPANS, PIECES, L], F32, name="own_weights")
-        nc.sync.dma_start(own_weights[:], wgt.rearrange("o (i p l) -> (o p) i l", i=PIECES, l=L))
+        own_entries = held.tile([P, HALF // P], F32, name="own_entries")
+        with nc.allow_non_contiguous_dma(reason="two kibibytes in all, and the first look-up needs them in this layout"):
+            nc.sync.dma_start(own_entries[:], wgt[:, :HALF].rearrange("o (q p) -> (o p) q", p=P))
+        own_weights = held.tile([SPANS, 2, L], F32, name="own_weights")
+        nc.scalar.dma_start(own_weights[:], wgt.rearrange("o (h p l) -> (o p) h l", h=2, l=L))
         states = held.tile([C, S], F32, name="states")
         nc.scalar.dma_start(states[:], x)
         offsets = held.tile([128, N // 16], U16, name="offsets")
@@ -45,51 +50,66 @@ def tile_pretrainedmodel_kernel(tc, x, wgt, w, b, offs, out):
         warm = held.tile([128, 1], F32, name="warm")
         nc.scalar.activation(warm[:], zero[:], mybir.ActivationFunctionType.Tanh)
 
-        identity = held.tile([SPANS, SPANS], F32, name="identity")
-        make_identity(nc, identity[:])
-        weights = []
-        for i in range(PIECES):
-            spread = psum_held.tile([C, SPANS, L], F32, name=f"spread{i}")
-            for l in range(L):
-                nc.tensor.transpose(
-                    spread[:, :, l], own_weights[:, i, l : l + 1].to_broadcast([SPANS, C]), identity[:]
-                )
-            row = held.tile([C, PIECE], F32, name=f"weights{i}")
-            if i == 0:
-                nc.vector.tensor_copy(row[:], spread[:].rearrange("c r l -> c (r l)"))
-            else:
-                nc.scalar.copy(row[:], spread[:].rearrange("c r l -> c (r l)"))
-            weights.append(row)
-
-        own_sum = held.tile([SPANS, PIECES], F32, name="own_sum")
+        own_sum = held.tile([SPANS, 2], F32, name="own_sum")
         nc.vector.tensor_reduce(own_sum[:], own_weights[:], innermost, add)
-        own_inv = held.tile([SPANS, PIECES], F32, name="own_inv")
+        own_inv = held.tile([SPANS, 2], F32, name="own_inv")
         nc.vector.reciprocal(own_inv[:], own_sum[:])
-        weight_inv = psum_held.tile([C, R], F32, name="weight_inv")
-        for i in range(PIECES):
-            nc.tensor.transpose(
-                weight_inv[:, i * SPANS : (i + 1) * SPANS],
-                own_inv[:, i : i + 1].to_broadcast([SPANS, C]),
-                identity[:],
-            )
+        own_share = held.tile([SPANS, L], F32, name="own_share")
+        nc.vector.tensor_scalar_mul(own_share[:], own_weights[:, 1, :], own_inv[:, 1:2])
 
-        picked = []
-        for i in range(PIECES):
-            product = held.tile([C, PIECE], F32, name=f"picked{i}")
+        identity = held.tile([P, P], F32, name="identity")
+        make_identity(nc, identity[:])
+        weights = held.tile([C, N], F32, name="weights")
+        for start, stop in FIRST_HALF:
+            spread = psum_held.tile([C, stop - start], F32, name=f"spread{start}")
+            for entry in range(start, stop, P):
+                q = entry // P
+                nc.tensor.transpose(
+                    spread[:, entry - start : entry - start + P], own_entries[:, q : q + 1].to_broadcast([P, C]), identity[:]
+                )
+            if start == 0:
+                nc.vector.tensor_copy(weights[:, start:stop], spread[:])
+            else:
+                nc.scalar.copy(weights[:, start:stop], spread[:])
+        shares = psum_held.tile([C, SPANS, L], F32, name="shares")
+        for l in range(L):
+            nc.tensor.transpose(shares[:, :, l], own_share[:, l : l + 1].to_broadcast([SPANS, C]), identity[:])
+        share_row = shares[:].rearrange("c r l -> c (r l)")
+        for start, stop in SECOND_HALF:
+            nc.scalar.copy(weights[:, start:stop], share_row[:, start - HALF : stop - HALF])
+        weight_inv = psum_held.tile([C, SPANS], F32, name="weight_inv")
+        nc.tensor.transpose(weight_inv[:], own_inv[:, 0:1].to_broadcast([SPANS, C]), identity[:])
+
+        parts = FIRST_HALF + SECOND_HALF
+        picked = held.tile([C, N], F32, name="picked")
+        total = held.tile([C, SPANS], F32, name="total")
+        feat = [held.tile([C, SPANS], BF16, name=f"feat{h}") for h in range(2)]
+
+        def look_up(start, stop):
             nc.vector.tensor_tensor(
-                product[:], states[:].indirect(offsets[:, i * PIECE // 16 : (i + 1) * PIECE // 16]), weights[i][:], mult
+                picked[:, start:stop], states[:].indirect(offsets[:, start // 16 : stop // 16]), weights[:, start:stop], mult
             )
-            picked.append(product)
 
-        for i in range(PIECES):
-            spans = slice(i * SPANS, (i + 1) * SPANS)
-            total = work.tile([C, SPANS], F32, name="total")
-            nc.vector.tensor_reduce(total[:], picked[i][:].rearrange("c (r l) -> c r l", l=L), innermost, add)
-            feat = work.tile([C, SPANS], BF16, name="feat")
-            nc.vector.tensor_tensor(feat[:], total[:], weight_inv[:, spans], mult)
+        def sum_spans(start, stop):
+            products = picked[:, start:stop].rearrange("c (r l) -> c r l", l=L)
+            if start < HALF:
+                nc.vector.tensor_reduce(total[:, start // L : stop // L], products, innermost, add)
+            else:
+                spans = slice((start - HALF) // L, (stop - HALF) // L)
+                with nc.allow_low_precision(reason="summed in float32 and rounded once, as the statement asks"):
+                    nc.vector.tensor_reduce(feat[1][:, spans], products, innermost, add)
 
+        look_up(*parts[0])
+        for before, part in zip(parts, parts[1:]):
+            look_up(*part)
+            sum_spans(*before)
+        nc.vector.tensor_tensor(feat[0][:], total[:], weight_inv[:], mult)
+        sum_spans(*parts[-1])
+
+        for h in range(2):
+            spans = slice(h * SPANS, (h + 1) * SPANS)
             logits = psum.tile([K, SPANS], F32, name="logits")
-            nc.tensor.matmul(logits[:], linear[:], feat[:], start=True, stop=True)
+            nc.tensor.matmul(logits[:], linear[:], feat[h][:], start=True, stop=True)
             squashed = work.tile([K, SPANS], F32, name="squashed")
             nc.scalar.activation(squashed[:], logits[:], mybir.ActivationFunctionType.Tanh, bias=bias[:], scale=1.0)
             scaled = work.tile([K, SPANS], F32, name="scaled")

@@ -14,9 +14,9 @@ K = 128
 AMP = 5.0
 SPANS = R // 2
 HALF = SPANS * L
+PART = 256
 P = 128
-FIRST_HALF = ((0, P), (P, 2 * P), (2 * P, 4 * P))
-SECOND_HALF = ((HALF, HALF + 2 * P), (HALF + 2 * P, HALF + 4 * P))
+M = PART // P
 
 FLOPS = 2 * C * K * R
 
@@ -31,9 +31,8 @@ def tile_pretrainedmodel_kernel(tc, x, wgt, w, b, offs, out):
         tc.psum_pool(name="psum", bufs=2) as psum,
         tc.psum_pool(name="psum_held", bufs=1) as psum_held,
     ):
-        own_entries = held.tile([P, HALF // P], F32, name="own_entries")
-        with nc.allow_non_contiguous_dma(reason="two kibibytes in all, and the first look-up needs them in this layout"):
-            nc.sync.dma_start(own_entries[:], wgt[:, :HALF].rearrange("o (q p) -> (o p) q", p=P))
+        own_entries = held.tile([P, HALF // PART, M], F32, name="own_entries")
+        nc.sync.dma_start(own_entries[:], wgt[:, :HALF].rearrange("o (i p m) -> (o p) i m", p=P, m=M))
         own_weights = held.tile([SPANS, 2, L], F32, name="own_weights")
         nc.scalar.dma_start(own_weights[:], wgt.rearrange("o (h p l) -> (o p) h l", h=2, l=L))
         states = held.tile([C, S], F32, name="states")
@@ -60,51 +59,49 @@ def tile_pretrainedmodel_kernel(tc, x, wgt, w, b, offs, out):
         identity = held.tile([P, P], F32, name="identity")
         make_identity(nc, identity[:])
         weights = held.tile([C, N], F32, name="weights")
-        for start, stop in FIRST_HALF:
-            spread = psum_held.tile([C, stop - start], F32, name=f"spread{start}")
-            for entry in range(start, stop, P):
-                q = entry // P
-                nc.tensor.transpose(
-                    spread[:, entry - start : entry - start + P], own_entries[:, q : q + 1].to_broadcast([P, C]), identity[:]
-                )
-            if start == 0:
-                nc.vector.tensor_copy(weights[:, start:stop], spread[:])
+        for i in range(HALF // PART):
+            spread = psum_held.tile([C, P, M], F32, name=f"spread{i}")
+            for m in range(M):
+                nc.tensor.transpose(spread[:, :, m], own_entries[:, i, m : m + 1].to_broadcast([P, C]), identity[:])
+            row = weights[:, i * PART : (i + 1) * PART]
+            if i == 0:
+                nc.vector.tensor_copy(row, spread[:].rearrange("c p m -> c (p m)"))
             else:
-                nc.scalar.copy(weights[:, start:stop], spread[:])
+                nc.scalar.copy(row, spread[:].rearrange("c p m -> c (p m)"))
         shares = psum_held.tile([C, SPANS, L], F32, name="shares")
         for l in range(L):
             nc.tensor.transpose(shares[:, :, l], own_share[:, l : l + 1].to_broadcast([SPANS, C]), identity[:])
         share_row = shares[:].rearrange("c r l -> c (r l)")
-        for start, stop in SECOND_HALF:
-            nc.scalar.copy(weights[:, start:stop], share_row[:, start - HALF : stop - HALF])
+        for start in range(0, HALF, PART):
+            nc.scalar.copy(weights[:, HALF + start : HALF + start + PART], share_row[:, start : start + PART])
         weight_inv = psum_held.tile([C, SPANS], F32, name="weight_inv")
         nc.tensor.transpose(weight_inv[:], own_inv[:, 0:1].to_broadcast([SPANS, C]), identity[:])
 
-        parts = FIRST_HALF + SECOND_HALF
         picked = held.tile([C, N], F32, name="picked")
-        total = held.tile([C, SPANS], F32, name="total")
-        feat = [held.tile([C, SPANS], BF16, name=f"feat{h}") for h in range(2)]
+        products = picked[:].rearrange("c (i r l) -> c i r l", i=N // PART, l=L)
 
-        def look_up(start, stop):
+        def look_up(i):
+            entries = slice(i * PART, (i + 1) * PART)
             nc.vector.tensor_tensor(
-                picked[:, start:stop], states[:].indirect(offsets[:, start // 16 : stop // 16]), weights[:, start:stop], mult
+                picked[:, entries],
+                states[:].indirect(offsets[:, entries.start // 16 : entries.stop // 16]),
+                weights[:, entries],
+                mult,
             )
 
-        def sum_spans(start, stop):
-            products = picked[:, start:stop].rearrange("c (r l) -> c r l", l=L)
-            if start < HALF:
-                nc.vector.tensor_reduce(total[:, start // L : stop // L], products, innermost, add)
-            else:
-                spans = slice((start - HALF) // L, (stop - HALF) // L)
-                with nc.allow_low_precision(reason="summed in float32 and rounded once, as the statement asks"):
-                    nc.vector.tensor_reduce(feat[1][:, spans], products, innermost, add)
-
-        look_up(*parts[0])
-        for before, part in zip(parts, parts[1:]):
-            look_up(*part)
-            sum_spans(*before)
-        nc.vector.tensor_tensor(feat[0][:], total[:], weight_inv[:], mult)
-        sum_spans(*parts[-1])
+        quarter = PART // L
+        total = held.tile([C, SPANS], F32, name="total")
+        feat = [held.tile([C, SPANS], BF16, name=f"feat{h}") for h in range(2)]
+        look_up(0)
+        look_up(1)
+        nc.vector.tensor_reduce(total[:, :quarter], products[:, 0], innermost, add)
+        look_up(2)
+        nc.vector.tensor_reduce(total[:, quarter:], products[:, 1], innermost, add)
+        look_up(3)
+        with nc.allow_low_precision(reason="summed in float32 and rounded once, as the statement asks"):
+            nc.vector.tensor_reduce(feat[1][:, :quarter], products[:, 2], innermost, add)
+            nc.vector.tensor_tensor(feat[0][:], total[:], weight_inv[:], mult)
+            nc.vector.tensor_reduce(feat[1][:, quarter:], products[:, 3], innermost, add)
 
         for h in range(2):
             spans = slice(h * SPANS, (h + 1) * SPANS)

@@ -60,20 +60,21 @@ def tile_pretrainedmodel_kernel(tc, x, wgt, w, b, offs, out):
         make_identity(nc, identity[:])
         weights = held.tile([C, N], F32, name="weights")
         for i in range(HALF // PART):
-            spread = psum_held.tile([C, P, M], F32, name=f"spread{i}")
+            spread = psum_held.tile([C, M, P], F32, name=f"spread{i}")
             for m in range(M):
-                nc.tensor.transpose(spread[:, :, m], own_entries[:, i, m : m + 1].to_broadcast([P, C]), identity[:])
-            row = weights[:, i * PART : (i + 1) * PART]
+                nc.tensor.transpose(spread[:, m, :], own_entries[:, i, m : m + 1].to_broadcast([P, C]), identity[:])
+            row = weights[:, i * PART : (i + 1) * PART].rearrange("c (p m) -> c p m", m=M)
             if i == 0:
-                nc.vector.tensor_copy(row, spread[:].rearrange("c p m -> c (p m)"))
+                nc.vector.tensor_copy(row, spread[:].rearrange("c m p -> c p m"))
             else:
-                nc.scalar.copy(row, spread[:].rearrange("c p m -> c (p m)"))
-        shares = psum_held.tile([C, SPANS, L], F32, name="shares")
+                nc.scalar.copy(row, spread[:].rearrange("c m p -> c p m"))
+        shares = psum_held.tile([C, L, SPANS], F32, name="shares")
         for l in range(L):
-            nc.tensor.transpose(shares[:, :, l], own_share[:, l : l + 1].to_broadcast([SPANS, C]), identity[:])
-        share_row = shares[:].rearrange("c r l -> c (r l)")
+            nc.tensor.transpose(shares[:, l, :], own_share[:, l : l + 1].to_broadcast([SPANS, C]), identity[:])
+        share_row = shares[:].rearrange("c l r -> c r l")
         for start in range(0, HALF, PART):
-            nc.scalar.copy(weights[:, HALF + start : HALF + start + PART], share_row[:, start : start + PART])
+            row = weights[:, HALF + start : HALF + start + PART].rearrange("c (r l) -> c r l", l=L)
+            nc.scalar.copy(row, share_row[:, start // L : (start + PART) // L, :])
         weight_inv = psum_held.tile([C, SPANS], F32, name="weight_inv")
         nc.tensor.transpose(weight_inv[:], own_inv[:, 0:1].to_broadcast([SPANS, C]), identity[:])
 

@@ -75,8 +75,10 @@ def tile_pretrainedmodel_kernel(tc, x, wgt, w, b, offs, out):
         for start in range(0, HALF, PART):
             row = weights[:, HALF + start : HALF + start + PART].rearrange("c (r l) -> c r l", l=L)
             nc.scalar.copy(row, share_row[:, start // L : (start + PART) // L, :])
-        weight_inv = psum_held.tile([C, SPANS], F32, name="weight_inv")
-        nc.tensor.transpose(weight_inv[:], own_inv[:, 0:1].to_broadcast([SPANS, C]), identity[:])
+        inv_spread = psum_held.tile([C, SPANS], F32, name="inv_spread")
+        nc.tensor.transpose(inv_spread[:], own_inv[:, 0:1].to_broadcast([SPANS, C]), identity[:])
+        weight_inv = held.tile([C, SPANS], F32, name="weight_inv")
+        nc.scalar.copy(weight_inv[:], inv_spread[:])
 
         picked = held.tile([C, N], F32, name="picked")
         products = picked[:].rearrange("c (i r l) -> c i r l", i=N // PART, l=L)
@@ -101,7 +103,7 @@ def tile_pretrainedmodel_kernel(tc, x, wgt, w, b, offs, out):
         look_up(3)
         with nc.allow_low_precision(reason="summed in float32 and rounded once, as the statement asks"):
             nc.vector.tensor_reduce(feat[1][:, :quarter], products[:, 2], innermost, add)
-            nc.vector.tensor_tensor(feat[0][:], total[:], weight_inv[:], mult)
+            nc.gpsimd.tensor_tensor(feat[0][:], total[:], weight_inv[:], mult)
             nc.vector.tensor_reduce(feat[1][:, quarter:], products[:, 3], innermost, add)
 
         for h in range(2):

import concourse.mybir as mybir
from concourse.masks import make_identity

F32 = mybir.dt.float32
BF16 = mybir.dt.bfloat16
U16 = mybir.dt.uint16

C = 128
S = 512
N = 1024
L = 4
R = N // L
K = 128
AMP = 5.0
SPANS = R // 2
HALF = SPANS * L
PART = 256
P = 128
M = PART // P

FLOPS = 2 * C * K * R


def tile_pretrainedmodel_kernel(tc, x, wgt, w, b, offs, out):
    nc = tc.nc
    mult, add = mybir.AluOpType.mult, mybir.AluOpType.add
    innermost = mybir.AxisListType.X
    with (
        tc.tile_pool(name="held", bufs=1) as held,
        tc.tile_pool(name="work", bufs=2) as work,
        tc.psum_pool(name="psum", bufs=2) as psum,
        tc.psum_pool(name="psum_held", bufs=1) as psum_held,
    ):
        own_entries = held.tile([P, HALF // PART, M], F32, name="own_entries")
        nc.sync.dma_start(own_entries[:], wgt[:, :HALF].rearrange("o (i p m) -> (o p) i m", p=P, m=M))
        own_weights = held.tile([SPANS, 2, L], F32, name="own_weights")
        nc.scalar.dma_start(own_weights[:], wgt.rearrange("o (h p l) -> (o p) h l", h=2, l=L))
        states = held.tile([C, S], F32, name="states")
        nc.scalar.dma_start(states[:], x)
        offsets = held.tile([128, N // 16], U16, name="offsets")
        nc.sync.dma_start(offsets[:], offs)
        linear = held.tile([C, K], BF16, name="linear")
        nc.sync.dma_start(linear[:], w)
        bias = held.tile([K, 1], F32, name="bias")
        nc.sync.dma_start(bias[:], b)

        zero = held.tile([128, 1], F32, name="zero")
        nc.vector.memset(zero[:], 0.0)
        warm = held.tile([128, 1], F32, name="warm")
        nc.scalar.activation(warm[:], zero[:], mybir.ActivationFunctionType.Tanh)

        own_sum = held.tile([SPANS, 2], F32, name="own_sum")
        nc.vector.tensor_reduce(own_sum[:], own_weights[:], innermost, add)
        own_inv = held.tile([SPANS, 2], F32, name="own_inv")
        nc.vector.reciprocal(own_inv[:], own_sum[:])
        own_share = held.tile([SPANS, L], F32, name="own_share")
        nc.vector.tensor_scalar_mul(own_share[:], own_weights[:, 1, :], own_inv[:, 1:2])

        identity = held.tile([P, P], F32, name="identity")
        make_identity(nc, identity[:])
        weights = held.tile([C, N], F32, name="weights")
        for i in range(HALF // PART):
            spread = psum_held.tile([C, M, P], F32, name=f"spread{i}")
            for m in range(M):
                nc.tensor.transpose(spread[:, m, :], own_entries[:, i, m : m + 1].to_broadcast([P, C]), identity[:])
            row = weights[:, i * PART : (i + 1) * PART].rearrange("c (p m) -> c p m", m=M)
            if i == 0:
                nc.vector.tensor_copy(row, spread[:].rearrange("c m p -> c p m"))
            else:
                nc.scalar.copy(row, spread[:].rearrange("c m p -> c p m"))
        shares = psum_held.tile([C, L, SPANS], F32, name="shares")
        for l in range(L):
            nc.tensor.transpose(shares[:, l, :], own_share[:, l : l + 1].to_broadcast([SPANS, C]), identity[:])
        share_row = shares[:].rearrange("c l r -> c r l")
        for start in range(0, HALF, PART):
            row = weights[:, HALF + start : HALF + start + PART].rearrange("c (r l) -> c r l", l=L)
            nc.scalar.copy(row, share_row[:, start // L : (start + PART) // L, :])
        inv_spread = psum_held.tile([C, SPANS], F32, name="inv_spread")
        nc.tensor.transpose(inv_spread[:], own_inv[:, 0:1].to_broadcast([SPANS, C]), identity[:])
        weight_inv = held.tile([C, SPANS], F32, name="weight_inv")
        nc.scalar.copy(weight_inv[:], inv_spread[:])

        picked = held.tile([C, N], F32, name="picked")
        products = picked[:].rearrange("c (i r l) -> c i r l", i=N // PART, l=L)

        def look_up(i):
            entries = slice(i * PART, (i + 1) * PART)
            nc.vector.tensor_tensor(
                picked[:, entries],
                states[:].indirect(offsets[:, entries.start // 16 : entries.stop // 16]),
                weights[:, entries],
                mult,
            )

        quarter = PART // L
        total = held.tile([C, SPANS], F32, name="total")
        feat = [held.tile([C, SPANS], BF16, name=f"feat{h}") for h in range(2)]
        look_up(0)
        look_up(1)
        nc.vector.tensor_reduce(total[:, :quarter], products[:, 0], innermost, add)
        look_up(2)
        nc.vector.tensor_reduce(total[:, quarter:], products[:, 1], innermost, add)
        look_up(3)
        with nc.allow_low_precision(reason="summed in float32 and rounded once, as the statement asks"):
            nc.vector.tensor_reduce(feat[1][:, :quarter], products[:, 2], innermost, add)
            nc.gpsimd.tensor_tensor(feat[0][:], total[:], weight_inv[:], mult)
            nc.vector.tensor_reduce(feat[1][:, quarter:], products[:, 3], innermost, add)

        for h in range(2):
            spans = slice(h * SPANS, (h + 1) * SPANS)
            logits = psum.tile([K, SPANS], F32, name="logits")
            nc.tensor.matmul(logits[:], linear[:], feat[h][:], start=True, stop=True)
            squashed = work.tile([K, SPANS], F32, name="squashed")
            nc.scalar.activation(squashed[:], logits[:], mybir.ActivationFunctionType.Tanh, bias=bias[:], scale=1.0)
            scaled = work.tile([K, SPANS], F32, name="scaled")
            nc.vector.tensor_scalar_mul(scaled[:], squashed[:], AMP)
            nc.sync.dma_start(out[:, spans], scaled[:])
